import numpy as np
import ml_dtypes


def mxq(x, axis, fmt="e4m3"):
    dtype, down = {"e4m3": (ml_dtypes.float8_e4m3fn, 7), "e5m2": (ml_dtypes.float8_e5m2, 14)}[fmt]
    v = np.moveaxis(np.asarray(x, np.float32).astype(ml_dtypes.bfloat16).astype(np.float64), axis, -1)
    blocks = v.reshape(v.shape[:-1] + (-1, 32))
    amax = np.abs(blocks).max(-1, keepdims=True)
    byte = np.maximum(np.where(amax > 0, np.frexp(amax)[1] - 1 + 127, 0) - down, 1)
    scale = np.exp2(byte - 127.0)
    codes = (blocks / scale).astype(np.float32).astype(dtype).astype(np.float64)
    return np.moveaxis((codes * scale).reshape(v.shape), -1, axis)


WIDE = False


def mx_kscale(k):
    if not WIDE:
        return np.ones(k)
    levels = np.array([10, -10, 5, -5, 0])
    a = np.random.permutation(np.resize(levels, k // 512 * 4)).reshape(k // 512, 4)
    idx = np.arange(k)
    return np.exp2(a[idx // 512, idx % 128 // 32])


BF16 = ml_dtypes.bfloat16


def bf(x):
    return np.asarray(x, np.float32).astype(BF16)


def f64(x):
    return np.asarray(x).astype(np.float64)


E2M1 = np.array([0.0, 0.5, 1.0, 1.5, 2.0, 3.0, 4.0, 6.0, -0.0, -0.5, -1.0, -1.5, -2.0, -3.0, -4.0, -6.0])


def pack_weight(w, fmt):
    k, n = w.shape
    w = f64(bf(w)).reshape(k // 32, 32, n)
    amax = np.abs(w).max(1)
    if fmt == "e4m3":
        byte = np.frexp(amax)[1] - 1 + 127 - 7
    else:
        mant, ex = np.frexp(amax / 6.0)
        byte = np.where(mant > 0.5, ex, ex - 1) + 127
    byte = np.clip(np.where(amax > 0, byte, 1), 1, 254)
    scaled = (w * np.exp2(127.0 - byte)[:, None, :]).reshape(k, n).astype(np.float32)
    by_word = np.ascontiguousarray(scaled.reshape(k // 512, 128, 4, n).transpose(0, 1, 3, 2))
    if fmt == "e4m3":
        words = by_word.astype(ml_dtypes.float8_e4m3fn).view(np.uint8)
    else:
        c = by_word.astype(ml_dtypes.float4_e2m1fn).view(np.uint8) & 0xF
        words = c[..., 0::2] | (c[..., 1::2] << 4)
    return np.ascontiguousarray(words), np.ascontiguousarray(byte.astype(np.uint8).reshape(k // 512, 16, n))


def unpack_weight(words, scales, fmt):
    g, p, n, _ = words.shape
    if fmt == "e4m3":
        vals = np.ascontiguousarray(words).view(ml_dtypes.float8_e4m3fn).astype(np.float64)
    else:
        nib = np.empty((g, p, n, 4), np.uint8)
        nib[..., 0::2] = words & 0xF
        nib[..., 1::2] = words >> 4
        vals = E2M1[nib]
    vals = vals * np.repeat(np.exp2(scales.astype(np.float64) - 127.0), 8, axis=1)[..., None]
    return vals.transpose(0, 1, 3, 2).reshape(g * 512, n)


B, C, H, W, S, HID, OC = 2, 2048, 16, 16, 2, 1024, 4096
H2, W2 = H // S, W // S
K1 = C * S * S
RESIDUAL = True
FMT = "e4m3"


def setup_inputs():
    s = mx_kscale(K1)
    s = s / s.max()
    sx = np.broadcast_to(s.reshape(C, 1, S, 1, S), (C, H2, S, W2, S)).reshape(C, H, W)
    x = bf(np.random.standard_normal((B, C, H, W)) * sx)
    w1 = np.random.standard_normal((HID, K1)) / np.sqrt(K1) / s
    weight1_words, weight1_scales = pack_weight(np.ascontiguousarray(w1.T), FMT)
    bias1 = bf(np.random.standard_normal(HID) * 0.2)
    w2 = np.random.standard_normal((OC, HID)) * 1.5 / np.sqrt(HID)
    weight2_words, weight2_scales = pack_weight(np.ascontiguousarray(w2.T), FMT)
    bias2 = bf(np.random.standard_normal(OC) * 0.2)
    return {"x": x,
            "weight1_words": weight1_words,
            "weight1_scales": weight1_scales,
            "bias1": bias1,
            "weight2_words": weight2_words,
            "weight2_scales": weight2_scales,
            "bias2": bias2}


def reference(x, weight1_words, weight1_scales, bias1, weight2_words, weight2_scales, bias2):
    x = f64(x)
    p = x.reshape(B, C, H2, S, W2, S)
    p = p.transpose(0, 2, 4, 1, 3, 5).reshape(B * H2 * W2, C * S * S)
    o1 = (mxq(p, 1, "e4m3") @ unpack_weight(weight1_words, weight1_scales, FMT)) + f64(bias1)
    o2 = o1 * (1.0 / (1.0 + np.exp(-o1)))
    o3 = (mxq(o2, 1, "e4m3") @ unpack_weight(weight2_words, weight2_scales, FMT)) + f64(bias2)
    out = o3.reshape(B, H2, W2, -1).transpose(0, 3, 1, 2)
    if RESIDUAL:
        pooled = x.reshape(B, C, H2, S, W2, S).mean(axis=(3, 5))
        n = out.shape[1] // C
        res = np.repeat(pooled, n, axis=1)
        out = out + res
    return out

@@ -1,0 +1,226 @@
+from contextlib import ExitStack
+
+import concourse.mybir as mybir
+from concourse.masks import make_identity
+
+F32 = mybir.dt.float32
+BF16 = mybir.dt.bfloat16
+I32 = mybir.dt.int32
+U8 = mybir.dt.uint8
+FP8X4 = mybir.dt.float8_e4m3fn_x4
+ADD = mybir.AluOpType.add
+ACT = mybir.ActivationFunctionType
+
+P = 128
+PACK = 4
+BANK = 512
+BATCH = 2
+CHANNELS = 2048
+PIXELS = 256
+SPOTS = 64
+HID = 1024
+OC = 4096
+PASSES1 = CHANNELS // P
+PASSES2 = HID // (P * PACK)
+QUAD = 4
+QUADS = PASSES1 // QUAD
+LIVE = 4
+W2_LOADS = 4
+CHUNKS = OC // BANK
+PAIRS = BANK // (2 * P)
+
+FLOPS = 2 * P * (CHANNELS * PACK) * HID + 2 * P * HID * OC
+
+
+def tile_memoryefficientpatchdownscale_k_kernel(
+    tc, x, weight1_words, weight1_scales, bias1, weight2_words, weight2_scales, bias2, out
+):
+    nc = tc.nc
+    with ExitStack() as ctx:
+        keep = ctx.enter_context(tc.tile_pool(name="keep", bufs=1))
+        work = ctx.enter_context(tc.tile_pool(name="work", bufs=2))
+        psum_o1 = ctx.enter_context(tc.psum_pool(name="psum_o1", bufs=1))
+        psum_small = ctx.enter_context(tc.psum_pool(name="psum_small", bufs=2))
+        psum_o3 = ctx.enter_context(tc.psum_pool(name="psum_o3", bufs=2))
+        psum_o3t = ctx.enter_context(tc.psum_pool(name="psum_o3t", bufs=2))
+        ctx.enter_context(tc.manual_schedule())
+
+        x_quads = [keep.tile([P, QUAD, BATCH, PIXELS], BF16, name="x_quad%d" % q) for q in range(QUADS)]
+        patches = [
+            keep.tile([P, QUAD * P * PACK], BF16, name="patches%d" % q, align_bytes=64) for q in range(QUADS)
+        ]
+        x_codes = keep.tile([P, PASSES1 * P], I32, align_bytes=64)
+        x_scales = keep.tile([P, PASSES1 * P], U8, align_bytes=64)
+        w1 = keep.tile([P, PASSES1, HID], I32, align_bytes=64)
+        w2 = keep.tile([P, PASSES2, OC], I32, align_bytes=64)
+        w1_scales = keep.tile([P, QUADS, HID], U8, align_bytes=64)
+        w2_scales = keep.tile([P, OC], U8, align_bytes=64)
+        bias1_row = keep.tile([P, HID], BF16)
+        bias2_rows = keep.tile([P, 2 * P], BF16)
+        ones = keep.tile([P, P], BF16)
+        ident_bf16 = keep.tile([P, P], BF16)
+        ident_f32 = keep.tile([P, P], F32)
+        bias1_all = keep.tile([P, PASSES2, PACK, P], F32)
+        bias2_cols = keep.tile([P, PASSES1, 2], F32)
+        zero_col = keep.tile([P, 1], F32)
+        silu_col = keep.tile([P, 1], F32)
+        patch_sums = keep.tile([P, PASSES1 * P], F32)
+        result = keep.tile([P, PASSES1, BATCH, 2, SPOTS], F32)
+        o2_codes = keep.tile([P, PASSES2 * P], I32, align_bytes=64)
+        o2_scales = keep.tile([P, PASSES2 * P], U8, align_bytes=64)
+
+        nc.vector.memset(w1_scales[:].rearrange("p q n -> p (q n)").bitcast(I32), 0)
+        nc.vector.memset(w2_scales[:].bitcast(I32), 0)
+        nc.vector.memset(zero_col[:], 0.0)
+        nc.gpsimd.memset(bias1_row[:], 0.0)
+        nc.gpsimd.memset(bias2_rows[:], 0.0)
+        nc.gpsimd.memset(ones[:], 1.0)
+        make_identity(nc, ident_bf16[:])
+        make_identity(nc, ident_f32[:])
+
+        nc.scalar.dma_start(out=bias1_row[0:1, :], in_=bias1.rearrange("(o n) -> o n", o=1))
+        nc.scalar.dma_start(out=bias2_rows[0:PASSES1, :], in_=bias2.rearrange("(g c) -> g c", c=2 * P))
+        nc.scalar.activation(out=silu_col[:], in_=zero_col[:], func=ACT.Silu)
+
+        x_by_channel = x.rearrange("b (g p) h w -> p g b (h w)", p=P)
+        for q in range(QUADS):
+            for b in range(BATCH):
+                nc.sync.dma_start(out=x_quads[q][:, :, b, :], in_=x_by_channel[:, QUAD * q : QUAD * (q + 1), b, :])
+        for q in range(QUADS):
+            for Q in range(4):
+                nc.sync.dma_start(
+                    out=w1_scales[32 * Q : 32 * Q + QUAD * LIVE, q, :].bitcast(I32),
+                    in_=weight1_scales[QUAD * q : QUAD * (q + 1), LIVE * Q : LIVE * (Q + 1), :].bitcast(I32),
+                )
+        for Q in range(4):
+            nc.sync.dma_start(
+                out=w2_scales[32 * Q : 32 * Q + PASSES2 * LIVE, :].bitcast(I32),
+                in_=weight2_scales[:, LIVE * Q : LIVE * (Q + 1), :].bitcast(I32),
+            )
+        for g in range(PASSES1):
+            nc.sync.dma_start(out=w1[:, g, :], in_=weight1_words[g].rearrange("p n t -> p (n t)").bitcast(I32))
+        w2_bytes = weight2_words.rearrange("g p n t -> p g (n t)")
+        w2_cols = OC // W2_LOADS
+        for n in range(W2_LOADS):
+            nc.sync.dma_start(
+                out=w2[:, :, w2_cols * n : w2_cols * (n + 1)],
+                in_=w2_bytes[:, :, PACK * w2_cols * n : PACK * w2_cols * (n + 1)].bitcast(I32),
+            )
+
+        for q in range(QUADS):
+            pixel_pairs = x_quads[q][:].rearrange("p g b f -> p (g b f)").bitcast(F32)
+            nc.vector.tensor_copy(
+                out=patches[q][:].bitcast(F32).rearrange("p (a j u) -> p a j u", j=8, u=2),
+                in_=pixel_pairs.rearrange("p (a u j) -> p a j u", u=2, j=8),
+            )
+            cols = slice(QUAD * P * q, QUAD * P * (q + 1))
+            nc.vector.quantize_mx(out=x_codes[:, cols].bitcast(FP8X4), scales=x_scales[:, cols], in_=patches[q][:])
+
+        for h in range(PASSES2):
+            bias1_ps = psum_small.tile([P, BANK], F32, tag="small")
+            nc.tensor.matmul(
+                out=bias1_ps[:], lhsT=ones[:], rhs=bias1_row[:, BANK * h : BANK * (h + 1)], start=True, stop=True
+            )
+            nc.scalar.copy(out=bias1_all[:, h, :, :], in_=bias1_ps[:].rearrange("m (p t) -> m t p", t=PACK))
+        bias2_ps = psum_small.tile([P, 2, P], BF16, tag="small")
+        for r in range(2):
+            nc.tensor.transpose(bias2_ps[:, r, :], bias2_rows[:, r : 2 * P : 2], ident_bf16[:])
+        nc.vector.tensor_copy(out=bias2_cols[:], in_=bias2_ps[:, :, 0:PASSES1].rearrange("p r g -> p g r"))
+
+        o1_ps = [psum_o1.tile([P, BANK], F32, name="o1_ps%d" % h) for h in range(PASSES2)]
+        for g in range(PASSES1):
+            first_row = LIVE * (g % QUAD)
+            for h in range(PASSES2):
+                cols = slice(BANK * h, BANK * (h + 1))
+                nc.tensor.matmul_mx(
+                    out=o1_ps[h][:],
+                    lhsT=x_codes[:, P * g : P * (g + 1)].bitcast(FP8X4),
+                    lhsT_scale=x_scales[:, P * g : P * (g + 1)],
+                    rhs=w1[:, g, cols].bitcast(FP8X4),
+                    rhs_scale=w1_scales[first_row:P, g // QUAD, cols],
+                    start=(g == 0),
+                    stop=(g == PASSES1 - 1),
+                )
+
+        for q in range(QUADS):
+            nc.vector.tensor_reduce(
+                out=patch_sums[:, QUAD * P * q : QUAD * P * (q + 1)],
+                in_=patches[q][:].rearrange("p (c t) -> p c t", t=PACK),
+                axis=mybir.AxisListType.X,
+                op=ADD,
+            )
+            for G in range(QUAD * q, QUAD * (q + 1)):
+                for r in range(2):
+                    nc.scalar.activation(
+                        out=result[:, G, :, r, :],
+                        in_=patch_sums[:, P * G : P * (G + 1)].rearrange("p (b s) -> p b s", b=BATCH),
+                        func=ACT.Identity,
+                        bias=bias2_cols[:, G, r : r + 1],
+                        scale=1.0 / PACK,
+                    )
+
+        for h in range(PASSES2):
+            o1_sorted = work.tile([P, PACK, P], F32)
+            nc.vector.tensor_tensor(
+                out=o1_sorted[:],
+                in0=o1_ps[h][:].rearrange("m (p t) -> m t p", t=PACK),
+                in1=bias1_all[:, h, :, :],
+                op=ADD,
+            )
+            o2_sorted = work.tile([P, PACK, P], BF16)
+            nc.scalar.activation(out=o2_sorted[:], in_=o1_sorted[:], func=ACT.Silu)
+            o2t_ps = psum_small.tile([P, PACK, P], BF16, tag="small")
+            for t in range(PACK):
+                nc.tensor.transpose(o2t_ps[:, t, :], o2_sorted[:, t, :], ident_bf16[:])
+            o2_words = work.tile([P, P, PACK], BF16, align_bytes=64)
+            nc.vector.tensor_copy(out=o2_words[:], in_=o2t_ps[:].rearrange("p t m -> p m t"))
+            nc.vector.quantize_mx(
+                out=o2_codes[:, P * h : P * (h + 1)].bitcast(FP8X4),
+                scales=o2_scales[:, P * h : P * (h + 1)],
+                in_=o2_words[:].rearrange("p m t -> p (m t)"),
+            )
+
+        out_by_pair = out.rearrange("b (g o r) i j -> o g b (r i j)", o=P, r=2)
+
+        def multiply(c):
+            o3_ps = psum_o3.tile([P, BANK], F32, name="o3_ps")
+            cols = slice(BANK * c, BANK * (c + 1))
+            for h in range(PASSES2):
+                nc.tensor.matmul_mx(
+                    out=o3_ps[:],
+                    lhsT=o2_codes[:, P * h : P * (h + 1)].bitcast(FP8X4),
+                    lhsT_scale=o2_scales[:, P * h : P * (h + 1)],
+                    rhs=w2[:, h, cols].bitcast(FP8X4),
+                    rhs_scale=w2_scales[LIVE * h : P, cols],
+                    start=(h == 0),
+                    stop=(h == PASSES2 - 1),
+                )
+            return o3_ps
+
+        def finish(c, o3_ps):
+            o3_sorted = work.tile([P, PAIRS, 2, P], F32, name="o3_sorted")
+            nc.scalar.copy(out=o3_sorted[:], in_=o3_ps[:].rearrange("m (a o r) -> m a r o", a=PAIRS, r=2))
+            o3t_ps = psum_o3t.tile([P, PAIRS, 2, P], F32, name="o3t_ps")
+            for a in range(PAIRS):
+                for r in range(2):
+                    nc.tensor.transpose(o3t_ps[:, a, r, :], o3_sorted[:, a, r, :], ident_f32[:])
+            for a in range(PAIRS):
+                G = PAIRS * c + a
+                nc.vector.tensor_tensor(
+                    out=result[:, G, :, :, :],
+                    in0=o3t_ps[:, a, :, :].rearrange("p r (b s) -> p b r s", b=BATCH),
+                    in1=result[:, G, :, :, :],
+                    op=ADD,
+                )
+            for b in range(BATCH):
+                nc.sync.dma_start(
+                    out=out_by_pair[:, PAIRS * c : PAIRS * (c + 1), b, :],
+                    in_=result[:, PAIRS * c : PAIRS * (c + 1), b, :, :].rearrange("p g r s -> p g (r s)"),
+                )
+
+        ahead = multiply(0)
+        for c in range(CHUNKS):
+            current = ahead
+            if c + 1 < CHUNKS:
+                ahead = multiply(c + 1)
+            finish(c, current)

@@ -92,13 +92,12 @@ def tile_memoryefficientpatchdownscale_k_kernel(
                     out=w1_scales[32 * Q : 32 * Q + QUAD * LIVE, q, :].bitcast(I32),
                     in_=weight1_scales[QUAD * q : QUAD * (q + 1), LIVE * Q : LIVE * (Q + 1), :].bitcast(I32),
                 )
-        for Q in range(4):
             nc.sync.dma_start(
-                out=w2_scales[32 * Q : 32 * Q + PASSES2 * LIVE, :].bitcast(I32),
-                in_=weight2_scales[:, LIVE * Q : LIVE * (Q + 1), :].bitcast(I32),
+                out=w2_scales[32 * q : 32 * q + PASSES2 * LIVE, :].bitcast(I32),
+                in_=weight2_scales[:, LIVE * q : LIVE * (q + 1), :].bitcast(I32),
             )
-        for g in range(PASSES1):
-            nc.sync.dma_start(out=w1[:, g, :], in_=weight1_words[g].rearrange("p n t -> p (n t)").bitcast(I32))
+            for g in range(QUAD * q, QUAD * (q + 1)):
+                nc.sync.dma_start(out=w1[:, g, :], in_=weight1_words[g].rearrange("p n t -> p (n t)").bitcast(I32))
         w2_bytes = weight2_words.rearrange("g p n t -> p g (n t)")
         w2_cols = OC // W2_LOADS
         for n in range(W2_LOADS):

@@ -28,6 +28,7 @@ LIVE = 4
 W2_LOADS = 4
 CHUNKS = OC // BANK
 PAIRS = BANK // (2 * P)
+RUN = 2
 
 FLOPS = 2 * P * (CHANNELS * PACK) * HID + 2 * P * HID * OC
 
@@ -39,10 +40,8 @@ def tile_memoryefficientpatchdownscale_k_kernel(
     with ExitStack() as ctx:
         keep = ctx.enter_context(tc.tile_pool(name="keep", bufs=1))
         work = ctx.enter_context(tc.tile_pool(name="work", bufs=2))
-        psum_o1 = ctx.enter_context(tc.psum_pool(name="psum_o1", bufs=1))
-        psum_small = ctx.enter_context(tc.psum_pool(name="psum_small", bufs=2))
-        psum_o3 = ctx.enter_context(tc.psum_pool(name="psum_o3", bufs=2))
-        psum_o3t = ctx.enter_context(tc.psum_pool(name="psum_o3t", bufs=2))
+        psum_mx = ctx.enter_context(tc.psum_pool(name="psum_mx", bufs=4))
+        psum_plain = ctx.enter_context(tc.psum_pool(name="psum_plain", bufs=4))
         ctx.enter_context(tc.manual_schedule())
 
         x_quads = [keep.tile([P, QUAD, BATCH, PIXELS], BF16, name="x_quad%d" % q) for q in range(QUADS)]
@@ -92,12 +91,13 @@ def tile_memoryefficientpatchdownscale_k_kernel(
                     out=w1_scales[32 * Q : 32 * Q + QUAD * LIVE, q, :].bitcast(I32),
                     in_=weight1_scales[QUAD * q : QUAD * (q + 1), LIVE * Q : LIVE * (Q + 1), :].bitcast(I32),
                 )
+        for Q in range(4):
             nc.sync.dma_start(
-                out=w2_scales[32 * q : 32 * q + PASSES2 * LIVE, :].bitcast(I32),
-                in_=weight2_scales[:, LIVE * q : LIVE * (q + 1), :].bitcast(I32),
+                out=w2_scales[32 * Q : 32 * Q + PASSES2 * LIVE, :].bitcast(I32),
+                in_=weight2_scales[:, LIVE * Q : LIVE * (Q + 1), :].bitcast(I32),
             )
-            for g in range(QUAD * q, QUAD * (q + 1)):
-                nc.sync.dma_start(out=w1[:, g, :], in_=weight1_words[g].rearrange("p n t -> p (n t)").bitcast(I32))
+        for g in range(PASSES1):
+            nc.sync.dma_start(out=w1[:, g, :], in_=weight1_words[g].rearrange("p n t -> p (n t)").bitcast(I32))
         w2_bytes = weight2_words.rearrange("g p n t -> p g (n t)")
         w2_cols = OC // W2_LOADS
         for n in range(W2_LOADS):
@@ -116,17 +116,17 @@ def tile_memoryefficientpatchdownscale_k_kernel(
             nc.vector.quantize_mx(out=x_codes[:, cols].bitcast(FP8X4), scales=x_scales[:, cols], in_=patches[q][:])
 
         for h in range(PASSES2):
-            bias1_ps = psum_small.tile([P, BANK], F32, tag="small")
+            bias1_ps = psum_plain.tile([P, BANK], F32, tag="plain")
             nc.tensor.matmul(
                 out=bias1_ps[:], lhsT=ones[:], rhs=bias1_row[:, BANK * h : BANK * (h + 1)], start=True, stop=True
             )
             nc.scalar.copy(out=bias1_all[:, h, :, :], in_=bias1_ps[:].rearrange("m (p t) -> m t p", t=PACK))
-        bias2_ps = psum_small.tile([P, 2, P], BF16, tag="small")
+        bias2_ps = psum_plain.tile([P, 2, P], BF16, tag="plain")
         for r in range(2):
             nc.tensor.transpose(bias2_ps[:, r, :], bias2_rows[:, r : 2 * P : 2], ident_bf16[:])
         nc.vector.tensor_copy(out=bias2_cols[:], in_=bias2_ps[:, :, 0:PASSES1].rearrange("p r g -> p g r"))
 
-        o1_ps = [psum_o1.tile([P, BANK], F32, name="o1_ps%d" % h) for h in range(PASSES2)]
+        o1_ps = [psum_mx.tile([P, BANK], F32, name="o1_ps%d" % h, tag="mx") for h in range(PASSES2)]
         for g in range(PASSES1):
             first_row = LIVE * (g % QUAD)
             for h in range(PASSES2):
@@ -158,31 +158,36 @@ def tile_memoryefficientpatchdownscale_k_kernel(
                         scale=1.0 / PACK,
                     )
 
-        for h in range(PASSES2):
-            o1_sorted = work.tile([P, PACK, P], F32)
+        halves = range(PASSES2)
+        o1_sorted = [work.tile([P, PACK, P], F32, name="o1_sorted") for h in halves]
+        o2_sorted = [work.tile([P, PACK, P], BF16, name="o2_sorted") for h in halves]
+        o2t_ps = [psum_plain.tile([P, PACK, P], BF16, name="o2t_ps", tag="plain") for h in halves]
+        o2_words = [work.tile([P, P, PACK], BF16, name="o2_words", align_bytes=64) for h in halves]
+        for h in halves:
             nc.vector.tensor_tensor(
-                out=o1_sorted[:],
+                out=o1_sorted[h][:],
                 in0=o1_ps[h][:].rearrange("m (p t) -> m t p", t=PACK),
                 in1=bias1_all[:, h, :, :],
                 op=ADD,
             )
-            o2_sorted = work.tile([P, PACK, P], BF16)
-            nc.scalar.activation(out=o2_sorted[:], in_=o1_sorted[:], func=ACT.Silu)
-            o2t_ps = psum_small.tile([P, PACK, P], BF16, tag="small")
+        for h in halves:
+            nc.scalar.activation(out=o2_sorted[h][:], in_=o1_sorted[h][:], func=ACT.Silu)
+        for h in halves:
             for t in range(PACK):
-                nc.tensor.transpose(o2t_ps[:, t, :], o2_sorted[:, t, :], ident_bf16[:])
-            o2_words = work.tile([P, P, PACK], BF16, align_bytes=64)
-            nc.vector.tensor_copy(out=o2_words[:], in_=o2t_ps[:].rearrange("p t m -> p m t"))
+                nc.tensor.transpose(o2t_ps[h][:, t, :], o2_sorted[h][:, t, :], ident_bf16[:])
+        for h in halves:
+            nc.vector.tensor_copy(out=o2_words[h][:], in_=o2t_ps[h][:].rearrange("p t m -> p m t"))
+        for h in halves:
             nc.vector.quantize_mx(
                 out=o2_codes[:, P * h : P * (h + 1)].bitcast(FP8X4),
                 scales=o2_scales[:, P * h : P * (h + 1)],
-                in_=o2_words[:].rearrange("p m t -> p (m t)"),
+                in_=o2_words[h][:].rearrange("p m t -> p (m t)"),
             )
 
         out_by_pair = out.rearrange("b (g o r) i j -> o g b (r i j)", o=P, r=2)
 
         def multiply(c):
-            o3_ps = psum_o3.tile([P, BANK], F32, name="o3_ps")
+            o3_ps = psum_mx.tile([P, BANK], F32, name="o3_ps", tag="mx")
             cols = slice(BANK * c, BANK * (c + 1))
             for h in range(PASSES2):
                 nc.tensor.matmul_mx(
@@ -197,9 +202,9 @@ def tile_memoryefficientpatchdownscale_k_kernel(
             return o3_ps
 
         def finish(c, o3_ps):
-            o3_sorted = work.tile([P, PAIRS, 2, P], F32, name="o3_sorted")
+            o3_sorted = work.tile([P, PAIRS, 2, P], F32, name="o3_sorted", bufs=2 * RUN)
             nc.scalar.copy(out=o3_sorted[:], in_=o3_ps[:].rearrange("m (a o r) -> m a r o", a=PAIRS, r=2))
-            o3t_ps = psum_o3t.tile([P, PAIRS, 2, P], F32, name="o3t_ps")
+            o3t_ps = psum_plain.tile([P, PAIRS, 2, P], F32, name="o3t_ps", tag="plain")
             for a in range(PAIRS):
                 for r in range(2):
                     nc.tensor.transpose(o3t_ps[:, a, r, :], o3_sorted[:, a, r, :], ident_f32[:])
@@ -217,9 +222,10 @@ def tile_memoryefficientpatchdownscale_k_kernel(
                     in_=result[:, PAIRS * c : PAIRS * (c + 1), b, :, :].rearrange("p g r s -> p g (r s)"),
                 )
 
-        ahead = multiply(0)
-        for c in range(CHUNKS):
+        ahead = [multiply(c) for c in range(RUN)]
+        for first in range(0, CHUNKS, RUN):
             current = ahead
-            if c + 1 < CHUNKS:
-                ahead = multiply(c + 1)
-            finish(c, current)
+            if first + RUN < CHUNKS:
+                ahead = [multiply(c) for c in range(first + RUN, first + 2 * RUN)]
+            for n in range(RUN):
+                finish(first + n, current[n])

@@ -71,9 +71,9 @@ def tile_memoryefficientpatchdownscale_k_kernel(
         nc.vector.memset(w1_scales[:].rearrange("p q n -> p (q n)").bitcast(I32), 0)
         nc.vector.memset(w2_scales[:].bitcast(I32), 0)
         nc.vector.memset(zero_col[:], 0.0)
-        nc.gpsimd.memset(bias1_row[:], 0.0)
-        nc.gpsimd.memset(bias2_rows[:], 0.0)
-        nc.gpsimd.memset(ones[:], 1.0)
+        nc.vector.memset(bias1_row[:], 0.0)
+        nc.vector.memset(bias2_rows[:], 0.0)
+        nc.vector.memset(ones[:], 1.0)
         make_identity(nc, ident_bf16[:])
         make_identity(nc, ident_f32[:])
 
@@ -85,17 +85,6 @@ def tile_memoryefficientpatchdownscale_k_kernel(
         for q in range(QUADS):
             for b in range(BATCH):
                 nc.sync.dma_start(out=x_quads[q][:, :, b, :], in_=x_by_channel[:, QUAD * q : QUAD * (q + 1), b, :])
-        for q in range(QUADS):
-            for Q in range(4):
-                nc.sync.dma_start(
-                    out=w1_scales[32 * Q : 32 * Q + QUAD * LIVE, q, :].bitcast(I32),
-                    in_=weight1_scales[QUAD * q : QUAD * (q + 1), LIVE * Q : LIVE * (Q + 1), :].bitcast(I32),
-                )
-        for Q in range(4):
-            nc.sync.dma_start(
-                out=w2_scales[32 * Q : 32 * Q + PASSES2 * LIVE, :].bitcast(I32),
-                in_=weight2_scales[:, LIVE * Q : LIVE * (Q + 1), :].bitcast(I32),
-            )
         for g in range(PASSES1):
             nc.sync.dma_start(out=w1[:, g, :], in_=weight1_words[g].rearrange("p n t -> p (n t)").bitcast(I32))
         w2_bytes = weight2_words.rearrange("g p n t -> p g (n t)")
@@ -104,6 +93,18 @@ def tile_memoryefficientpatchdownscale_k_kernel(
             nc.sync.dma_start(
                 out=w2[:, :, w2_cols * n : w2_cols * (n + 1)],
                 in_=w2_bytes[:, :, PACK * w2_cols * n : PACK * w2_cols * (n + 1)].bitcast(I32),
+            )
+
+        for q in range(QUADS):
+            for Q in range(4):
+                nc.gpsimd.dma_start(
+                    out=w1_scales[32 * Q : 32 * Q + QUAD * LIVE, q, :].bitcast(F32),
+                    in_=weight1_scales[QUAD * q : QUAD * (q + 1), LIVE * Q : LIVE * (Q + 1), :].bitcast(F32),
+                )
+        for Q in range(4):
+            nc.gpsimd.dma_start(
+                out=w2_scales[32 * Q : 32 * Q + PASSES2 * LIVE, :].bitcast(F32),
+                in_=weight2_scales[:, LIVE * Q : LIVE * (Q + 1), :].bitcast(F32),
             )
 
         for q in range(QUADS):

@@ -25,10 +25,12 @@ PASSES2 = HID // (P * PACK)
 QUAD = 4
 QUADS = PASSES1 // QUAD
 LIVE = 4
-W2_LOADS = 4
-CHUNKS = OC // BANK
-PAIRS = BANK // (2 * P)
-RUN = 2
+TWINS = OC // CHANNELS
+RUN_BANKS = 2
+RUN_COLS = RUN_BANKS * BANK
+RUNS = OC // RUN_COLS
+OCTET = RUN_COLS // P
+RESIDUAL_STEP = 3
 
 FLOPS = 2 * P * (CHANNELS * PACK) * HID + 2 * P * HID * OC
 
@@ -48,6 +50,7 @@ def tile_memoryefficientpatchdownscale_k_kernel(
         patches = [
             keep.tile([P, QUAD * P * PACK], BF16, name="patches%d" % q, align_bytes=64) for q in range(QUADS)
         ]
+        by_channel = [keep.tile([P, TWINS, QUAD, P], F32, name="by_channel%d" % q) for q in range(QUADS)]
         x_codes = keep.tile([P, PASSES1 * P], I32, align_bytes=64)
         x_scales = keep.tile([P, PASSES1 * P], U8, align_bytes=64)
         w1 = keep.tile([P, PASSES1, HID], I32, align_bytes=64)
@@ -55,16 +58,15 @@ def tile_memoryefficientpatchdownscale_k_kernel(
         w1_scales = keep.tile([P, QUADS, HID], U8, align_bytes=64)
         w2_scales = keep.tile([P, OC], U8, align_bytes=64)
         bias1_row = keep.tile([P, HID], BF16)
-        bias2_rows = keep.tile([P, 2 * P], BF16)
+        bias2_rows = keep.tile([P, TWINS * P], BF16)
         ones = keep.tile([P, P], BF16)
         ident_bf16 = keep.tile([P, P], BF16)
         ident_f32 = keep.tile([P, P], F32)
         bias1_all = keep.tile([P, PASSES2, PACK, P], F32)
-        bias2_cols = keep.tile([P, PASSES1, 2], F32)
+        bias2_cols = keep.tile([P, PASSES1, TWINS], F32)
         zero_col = keep.tile([P, 1], F32)
         silu_col = keep.tile([P, 1], F32)
-        patch_sums = keep.tile([P, PASSES1 * P], F32)
-        result = keep.tile([P, PASSES1, BATCH, 2, SPOTS], F32)
+        addend = keep.tile([P, RUNS, OCTET, P], F32)
         o2_codes = keep.tile([P, PASSES2 * P], I32, align_bytes=64)
         o2_scales = keep.tile([P, PASSES2 * P], U8, align_bytes=64)
 
@@ -78,7 +80,7 @@ def tile_memoryefficientpatchdownscale_k_kernel(
         make_identity(nc, ident_f32[:])
 
         nc.scalar.dma_start(out=bias1_row[0:1, :], in_=bias1.rearrange("(o n) -> o n", o=1))
-        nc.scalar.dma_start(out=bias2_rows[0:PASSES1, :], in_=bias2.rearrange("(g c) -> g c", c=2 * P))
+        nc.scalar.dma_start(out=bias2_rows[0:PASSES1, :], in_=bias2.rearrange("(g c) -> g c", c=TWINS * P))
         nc.scalar.activation(out=silu_col[:], in_=zero_col[:], func=ACT.Silu)
 
         x_by_channel = x.rearrange("b (g p) h w -> p g b (h w)", p=P)
@@ -88,11 +90,10 @@ def tile_memoryefficientpatchdownscale_k_kernel(
         for g in range(PASSES1):
             nc.sync.dma_start(out=w1[:, g, :], in_=weight1_words[g].rearrange("p n t -> p (n t)").bitcast(I32))
         w2_bytes = weight2_words.rearrange("g p n t -> p g (n t)")
-        w2_cols = OC // W2_LOADS
-        for n in range(W2_LOADS):
+        for n in range(RUNS):
             nc.sync.dma_start(
-                out=w2[:, :, w2_cols * n : w2_cols * (n + 1)],
-                in_=w2_bytes[:, :, PACK * w2_cols * n : PACK * w2_cols * (n + 1)].bitcast(I32),
+                out=w2[:, :, RUN_COLS * n : RUN_COLS * (n + 1)],
+                in_=w2_bytes[:, :, PACK * RUN_COLS * n : PACK * RUN_COLS * (n + 1)].bitcast(I32),
             )
 
         for q in range(QUADS):
@@ -107,6 +108,17 @@ def tile_memoryefficientpatchdownscale_k_kernel(
                 in_=weight2_scales[:, LIVE * Q : LIVE * (Q + 1), :].bitcast(F32),
             )
 
+        for h in range(PASSES2):
+            bias1_ps = psum_plain.tile([P, BANK], F32, tag="plain")
+            nc.tensor.matmul(
+                out=bias1_ps[:], lhsT=ones[:], rhs=bias1_row[:, BANK * h : BANK * (h + 1)], start=True, stop=True
+            )
+            nc.scalar.copy(out=bias1_all[:, h, :, :], in_=bias1_ps[:].rearrange("m (p t) -> m t p", t=PACK))
+        bias2_ps = psum_plain.tile([P, TWINS, P], BF16, tag="plain")
+        for e in range(TWINS):
+            nc.tensor.transpose(bias2_ps[:, e, :], bias2_rows[:, e : TWINS * P : TWINS], ident_bf16[:])
+        nc.scalar.copy(out=bias2_cols[:], in_=bias2_ps[:, :, 0:PASSES1].rearrange("p e g -> p g e"))
+
         for q in range(QUADS):
             pixel_pairs = x_quads[q][:].rearrange("p g b f -> p (g b f)").bitcast(F32)
             nc.vector.tensor_copy(
@@ -115,17 +127,32 @@ def tile_memoryefficientpatchdownscale_k_kernel(
             )
             cols = slice(QUAD * P * q, QUAD * P * (q + 1))
             nc.vector.quantize_mx(out=x_codes[:, cols].bitcast(FP8X4), scales=x_scales[:, cols], in_=patches[q][:])
-
-        for h in range(PASSES2):
-            bias1_ps = psum_plain.tile([P, BANK], F32, tag="plain")
-            nc.tensor.matmul(
-                out=bias1_ps[:], lhsT=ones[:], rhs=bias1_row[:, BANK * h : BANK * (h + 1)], start=True, stop=True
+            patch_sums = work.tile([P, QUAD, P], F32)
+            nc.vector.tensor_reduce(
+                out=patch_sums[:].rearrange("p a m -> p (a m)"),
+                in_=patches[q][:].rearrange("p (c t) -> p c t", t=PACK),
+                axis=mybir.AxisListType.X,
+                op=ADD,
             )
-            nc.scalar.copy(out=bias1_all[:, h, :, :], in_=bias1_ps[:].rearrange("m (p t) -> m t p", t=PACK))
-        bias2_ps = psum_plain.tile([P, 2, P], BF16, tag="plain")
-        for r in range(2):
-            nc.tensor.transpose(bias2_ps[:, r, :], bias2_rows[:, r : 2 * P : 2], ident_bf16[:])
-        nc.vector.tensor_copy(out=bias2_cols[:], in_=bias2_ps[:, :, 0:PASSES1].rearrange("p r g -> p g r"))
+            for a in range(QUAD):
+                for e in range(TWINS):
+                    nc.scalar.activation(
+                        out=by_channel[q][:, e, a, :],
+                        in_=patch_sums[:, a, :],
+                        func=ACT.Identity,
+                        bias=bias2_cols[:, QUAD * q + a, e : e + 1],
+                        scale=1.0 / PACK,
+                    )
+
+        def transpose_residual(q):
+            for e in range(TWINS):
+                by_patch = psum_plain.tile([P, QUAD, P], F32, name="by_patch", tag="plain")
+                for a in range(QUAD):
+                    nc.tensor.transpose(by_patch[:, a, :], by_channel[q][:, e, a, :], ident_f32[:])
+                nc.vector.tensor_copy(
+                    out=addend[:, q, e:OCTET:TWINS, :].rearrange("m w (a v) -> m w a v", a=QUAD),
+                    in_=by_patch[:].rearrange("m a (v w) -> m w a v", w=OCTET // TWINS),
+                )
 
         o1_ps = [psum_mx.tile([P, BANK], F32, name="o1_ps%d" % h, tag="mx") for h in range(PASSES2)]
         for g in range(PASSES1):
@@ -141,23 +168,8 @@ def tile_memoryefficientpatchdownscale_k_kernel(
                     start=(g == 0),
                     stop=(g == PASSES1 - 1),
                 )
-
-        for q in range(QUADS):
-            nc.vector.tensor_reduce(
-                out=patch_sums[:, QUAD * P * q : QUAD * P * (q + 1)],
-                in_=patches[q][:].rearrange("p (c t) -> p c t", t=PACK),
-                axis=mybir.AxisListType.X,
-                op=ADD,
-            )
-            for G in range(QUAD * q, QUAD * (q + 1)):
-                for r in range(2):
-                    nc.scalar.activation(
-                        out=result[:, G, :, r, :],
-                        in_=patch_sums[:, P * G : P * (G + 1)].rearrange("p (b s) -> p b s", b=BATCH),
-                        func=ACT.Identity,
-                        bias=bias2_cols[:, G, r : r + 1],
-                        scale=1.0 / PACK,
-                    )
+            if g % RESIDUAL_STEP == RESIDUAL_STEP - 1 and g // RESIDUAL_STEP < QUADS:
+                transpose_residual(g // RESIDUAL_STEP)
 
         halves = range(PASSES2)
         o1_sorted = [work.tile([P, PACK, P], F32, name="o1_sorted") for h in halves]
@@ -185,11 +197,11 @@ def tile_memoryefficientpatchdownscale_k_kernel(
                 in_=o2_words[h][:].rearrange("p m t -> p (m t)"),
             )
 
-        out_by_pair = out.rearrange("b (g o r) i j -> o g b (r i j)", o=P, r=2)
+        out_by_octet = out.rearrange("b (n p r) i j -> p n b (r i j)", p=P, r=OCTET)
 
-        def multiply(c):
+        def multiply(n, k):
             o3_ps = psum_mx.tile([P, BANK], F32, name="o3_ps", tag="mx")
-            cols = slice(BANK * c, BANK * (c + 1))
+            cols = slice(RUN_COLS * n + BANK * k, RUN_COLS * n + BANK * (k + 1))
             for h in range(PASSES2):
                 nc.tensor.matmul_mx(
                     out=o3_ps[:],
@@ -202,31 +214,29 @@ def tile_memoryefficientpatchdownscale_k_kernel(
                 )
             return o3_ps
 
-        def finish(c, o3_ps):
-            o3_sorted = work.tile([P, PAIRS, 2, P], F32, name="o3_sorted", bufs=2 * RUN)
-            nc.scalar.copy(out=o3_sorted[:], in_=o3_ps[:].rearrange("m (a o r) -> m a r o", a=PAIRS, r=2))
-            o3t_ps = psum_plain.tile([P, PAIRS, 2, P], F32, name="o3t_ps", tag="plain")
-            for a in range(PAIRS):
-                for r in range(2):
-                    nc.tensor.transpose(o3t_ps[:, a, r, :], o3_sorted[:, a, r, :], ident_f32[:])
-            for a in range(PAIRS):
-                G = PAIRS * c + a
+        def finish(n, banks):
+            share = BANK // OCTET
+            for k in range(RUN_BANKS):
+                total = addend[:, n, :, share * k : share * (k + 1)]
                 nc.vector.tensor_tensor(
-                    out=result[:, G, :, :, :],
-                    in0=o3t_ps[:, a, :, :].rearrange("p r (b s) -> p b r s", b=BATCH),
-                    in1=result[:, G, :, :, :],
-                    op=ADD,
+                    out=total, in0=banks[k][:].rearrange("m (p r) -> m r p", r=OCTET), in1=total, op=ADD
+                )
+            result = work.tile([P, BATCH, OCTET, SPOTS], F32, name="result")
+            planes = BANK // P
+            for k in range(RUN_BANKS):
+                o3t_ps = psum_plain.tile([P, planes, P], F32, name="o3t_ps", tag="plain")
+                for r in range(planes):
+                    nc.tensor.transpose(o3t_ps[:, r, :], addend[:, n, planes * k + r, :], ident_f32[:])
+                nc.scalar.copy(
+                    out=result[:, :, planes * k : planes * (k + 1), :],
+                    in_=o3t_ps[:].rearrange("p r (b s) -> p b r s", b=BATCH),
                 )
             for b in range(BATCH):
-                nc.sync.dma_start(
-                    out=out_by_pair[:, PAIRS * c : PAIRS * (c + 1), b, :],
-                    in_=result[:, PAIRS * c : PAIRS * (c + 1), b, :, :].rearrange("p g r s -> p g (r s)"),
-                )
+                nc.sync.dma_start(out=out_by_octet[:, n, b, :], in_=result[:, b, :, :].rearrange("p r s -> p (r s)"))
 
-        ahead = [multiply(c) for c in range(RUN)]
-        for first in range(0, CHUNKS, RUN):
+        ahead = [multiply(0, k) for k in range(RUN_BANKS)]
+        for n in range(RUNS):
             current = ahead
-            if first + RUN < CHUNKS:
-                ahead = [multiply(c) for c in range(first + RUN, first + 2 * RUN)]
-            for n in range(RUN):
-                finish(first + n, current[n])
+            if n + 1 < RUNS:
+                ahead = [multiply(n + 1, k) for k in range(RUN_BANKS)]
+            finish(n, current)

@@ -25,12 +25,10 @@ PASSES2 = HID // (P * PACK)
 QUAD = 4
 QUADS = PASSES1 // QUAD
 LIVE = 4
-TWINS = OC // CHANNELS
-RUN_BANKS = 2
-RUN_COLS = RUN_BANKS * BANK
-RUNS = OC // RUN_COLS
-OCTET = RUN_COLS // P
-RESIDUAL_STEP = 3
+W2_LOADS = 4
+CHUNKS = OC // BANK
+PAIRS = BANK // (2 * P)
+RUN = 2
 
 FLOPS = 2 * P * (CHANNELS * PACK) * HID + 2 * P * HID * OC
 
@@ -50,7 +48,6 @@ def tile_memoryefficientpatchdownscale_k_kernel(
         patches = [
             keep.tile([P, QUAD * P * PACK], BF16, name="patches%d" % q, align_bytes=64) for q in range(QUADS)
         ]
-        by_channel = [keep.tile([P, TWINS, QUAD, P], F32, name="by_channel%d" % q) for q in range(QUADS)]
         x_codes = keep.tile([P, PASSES1 * P], I32, align_bytes=64)
         x_scales = keep.tile([P, PASSES1 * P], U8, align_bytes=64)
         w1 = keep.tile([P, PASSES1, HID], I32, align_bytes=64)
@@ -58,15 +55,16 @@ def tile_memoryefficientpatchdownscale_k_kernel(
         w1_scales = keep.tile([P, QUADS, HID], U8, align_bytes=64)
         w2_scales = keep.tile([P, OC], U8, align_bytes=64)
         bias1_row = keep.tile([P, HID], BF16)
-        bias2_rows = keep.tile([P, TWINS * P], BF16)
+        bias2_rows = keep.tile([P, 2 * P], BF16)
         ones = keep.tile([P, P], BF16)
         ident_bf16 = keep.tile([P, P], BF16)
         ident_f32 = keep.tile([P, P], F32)
         bias1_all = keep.tile([P, PASSES2, PACK, P], F32)
-        bias2_cols = keep.tile([P, PASSES1, TWINS], F32)
+        bias2_cols = keep.tile([P, PASSES1, 2], F32)
         zero_col = keep.tile([P, 1], F32)
         silu_col = keep.tile([P, 1], F32)
-        addend = keep.tile([P, RUNS, OCTET, P], F32)
+        patch_sums = keep.tile([P, PASSES1 * P], F32)
+        result = keep.tile([P, PASSES1, BATCH, 2, SPOTS], F32)
         o2_codes = keep.tile([P, PASSES2 * P], I32, align_bytes=64)
         o2_scales = keep.tile([P, PASSES2 * P], U8, align_bytes=64)
 
@@ -80,7 +78,7 @@ def tile_memoryefficientpatchdownscale_k_kernel(
         make_identity(nc, ident_f32[:])
 
         nc.scalar.dma_start(out=bias1_row[0:1, :], in_=bias1.rearrange("(o n) -> o n", o=1))
-        nc.scalar.dma_start(out=bias2_rows[0:PASSES1, :], in_=bias2.rearrange("(g c) -> g c", c=TWINS * P))
+        nc.scalar.dma_start(out=bias2_rows[0:PASSES1, :], in_=bias2.rearrange("(g c) -> g c", c=2 * P))
         nc.scalar.activation(out=silu_col[:], in_=zero_col[:], func=ACT.Silu)
 
         x_by_channel = x.rearrange("b (g p) h w -> p g b (h w)", p=P)
@@ -90,10 +88,11 @@ def tile_memoryefficientpatchdownscale_k_kernel(
         for g in range(PASSES1):
             nc.sync.dma_start(out=w1[:, g, :], in_=weight1_words[g].rearrange("p n t -> p (n t)").bitcast(I32))
         w2_bytes = weight2_words.rearrange("g p n t -> p g (n t)")
-        for n in range(RUNS):
+        w2_cols = OC // W2_LOADS
+        for n in range(W2_LOADS):
             nc.sync.dma_start(
-                out=w2[:, :, RUN_COLS * n : RUN_COLS * (n + 1)],
-                in_=w2_bytes[:, :, PACK * RUN_COLS * n : PACK * RUN_COLS * (n + 1)].bitcast(I32),
+                out=w2[:, :, w2_cols * n : w2_cols * (n + 1)],
+                in_=w2_bytes[:, :, PACK * w2_cols * n : PACK * w2_cols * (n + 1)].bitcast(I32),
             )
 
         for q in range(QUADS):
@@ -108,17 +107,6 @@ def tile_memoryefficientpatchdownscale_k_kernel(
                 in_=weight2_scales[:, LIVE * Q : LIVE * (Q + 1), :].bitcast(F32),
             )
 
-        for h in range(PASSES2):
-            bias1_ps = psum_plain.tile([P, BANK], F32, tag="plain")
-            nc.tensor.matmul(
-                out=bias1_ps[:], lhsT=ones[:], rhs=bias1_row[:, BANK * h : BANK * (h + 1)], start=True, stop=True
-            )
-            nc.scalar.copy(out=bias1_all[:, h, :, :], in_=bias1_ps[:].rearrange("m (p t) -> m t p", t=PACK))
-        bias2_ps = psum_plain.tile([P, TWINS, P], BF16, tag="plain")
-        for e in range(TWINS):
-            nc.tensor.transpose(bias2_ps[:, e, :], bias2_rows[:, e : TWINS * P : TWINS], ident_bf16[:])
-        nc.scalar.copy(out=bias2_cols[:], in_=bias2_ps[:, :, 0:PASSES1].rearrange("p e g -> p g e"))
-
         for q in range(QUADS):
             pixel_pairs = x_quads[q][:].rearrange("p g b f -> p (g b f)").bitcast(F32)
             nc.vector.tensor_copy(
@@ -127,32 +115,17 @@ def tile_memoryefficientpatchdownscale_k_kernel(
             )
             cols = slice(QUAD * P * q, QUAD * P * (q + 1))
             nc.vector.quantize_mx(out=x_codes[:, cols].bitcast(FP8X4), scales=x_scales[:, cols], in_=patches[q][:])
-            patch_sums = work.tile([P, QUAD, P], F32)
-            nc.vector.tensor_reduce(
-                out=patch_sums[:].rearrange("p a m -> p (a m)"),
-                in_=patches[q][:].rearrange("p (c t) -> p c t", t=PACK),
-                axis=mybir.AxisListType.X,
-                op=ADD,
-            )
-            for a in range(QUAD):
-                for e in range(TWINS):
-                    nc.scalar.activation(
-                        out=by_channel[q][:, e, a, :],
-                        in_=patch_sums[:, a, :],
-                        func=ACT.Identity,
-                        bias=bias2_cols[:, QUAD * q + a, e : e + 1],
-                        scale=1.0 / PACK,
-                    )
 
-        def transpose_residual(q):
-            for e in range(TWINS):
-                by_patch = psum_plain.tile([P, QUAD, P], F32, name="by_patch", tag="plain")
-                for a in range(QUAD):
-                    nc.tensor.transpose(by_patch[:, a, :], by_channel[q][:, e, a, :], ident_f32[:])
-                nc.vector.tensor_copy(
-                    out=addend[:, q, e:OCTET:TWINS, :].rearrange("m w (a v) -> m w a v", a=QUAD),
-                    in_=by_patch[:].rearrange("m a (v w) -> m w a v", w=OCTET // TWINS),
-                )
+        for h in range(PASSES2):
+            bias1_ps = psum_plain.tile([P, BANK], F32, tag="plain")
+            nc.tensor.matmul(
+                out=bias1_ps[:], lhsT=ones[:], rhs=bias1_row[:, BANK * h : BANK * (h + 1)], start=True, stop=True
+            )
+            nc.scalar.copy(out=bias1_all[:, h, :, :], in_=bias1_ps[:].rearrange("m (p t) -> m t p", t=PACK))
+        bias2_ps = psum_plain.tile([P, 2, P], BF16, tag="plain")
+        for r in range(2):
+            nc.tensor.transpose(bias2_ps[:, r, :], bias2_rows[:, r : 2 * P : 2], ident_bf16[:])
+        nc.vector.tensor_copy(out=bias2_cols[:], in_=bias2_ps[:, :, 0:PASSES1].rearrange("p r g -> p g r"))
 
         o1_ps = [psum_mx.tile([P, BANK], F32, name="o1_ps%d" % h, tag="mx") for h in range(PASSES2)]
         for g in range(PASSES1):
@@ -168,8 +141,23 @@ def tile_memoryefficientpatchdownscale_k_kernel(
                     start=(g == 0),
                     stop=(g == PASSES1 - 1),
                 )
-            if g % RESIDUAL_STEP == RESIDUAL_STEP - 1 and g // RESIDUAL_STEP < QUADS:
-                transpose_residual(g // RESIDUAL_STEP)
+
+        for q in range(QUADS):
+            nc.vector.tensor_reduce(
+                out=patch_sums[:, QUAD * P * q : QUAD * P * (q + 1)],
+                in_=patches[q][:].rearrange("p (c t) -> p c t", t=PACK),
+                axis=mybir.AxisListType.X,
+                op=ADD,
+            )
+            for G in range(QUAD * q, QUAD * (q + 1)):
+                for r in range(2):
+                    nc.scalar.activation(
+                        out=result[:, G, :, r, :],
+                        in_=patch_sums[:, P * G : P * (G + 1)].rearrange("p (b s) -> p b s", b=BATCH),
+                        func=ACT.Identity,
+                        bias=bias2_cols[:, G, r : r + 1],
+                        scale=1.0 / PACK,
+                    )
 
         halves = range(PASSES2)
         o1_sorted = [work.tile([P, PACK, P], F32, name="o1_sorted") for h in halves]
@@ -190,53 +178,50 @@ def tile_memoryefficientpatchdownscale_k_kernel(
                 nc.tensor.transpose(o2t_ps[h][:, t, :], o2_sorted[h][:, t, :], ident_bf16[:])
         for h in halves:
             nc.vector.tensor_copy(out=o2_words[h][:], in_=o2t_ps[h][:].rearrange("p t m -> p m t"))
-        for h in halves:
             nc.vector.quantize_mx(
                 out=o2_codes[:, P * h : P * (h + 1)].bitcast(FP8X4),
                 scales=o2_scales[:, P * h : P * (h + 1)],
                 in_=o2_words[h][:].rearrange("p m t -> p (m t)"),
             )
 
-        out_by_octet = out.rearrange("b (n p r) i j -> p n b (r i j)", p=P, r=OCTET)
+        out_by_pair = out.rearrange("b (g o r) i j -> o g b (r i j)", o=P, r=2)
 
-        def multiply(n, k):
-            o3_ps = psum_mx.tile([P, BANK], F32, name="o3_ps", tag="mx")
-            cols = slice(RUN_COLS * n + BANK * k, RUN_COLS * n + BANK * (k + 1))
+        def multiply(chunks):
+            banks = [psum_mx.tile([P, BANK], F32, name="o3_ps", tag="mx") for c in chunks]
             for h in range(PASSES2):
-                nc.tensor.matmul_mx(
-                    out=o3_ps[:],
-                    lhsT=o2_codes[:, P * h : P * (h + 1)].bitcast(FP8X4),
-                    lhsT_scale=o2_scales[:, P * h : P * (h + 1)],
-                    rhs=w2[:, h, cols].bitcast(FP8X4),
-                    rhs_scale=w2_scales[LIVE * h : P, cols],
-                    start=(h == 0),
-                    stop=(h == PASSES2 - 1),
-                )
-            return o3_ps
+                for c, o3_ps in zip(chunks, banks):
+                    cols = slice(BANK * c, BANK * (c + 1))
+                    nc.tensor.matmul_mx(
+                        out=o3_ps[:],
+                        lhsT=o2_codes[:, P * h : P * (h + 1)].bitcast(FP8X4),
+                        lhsT_scale=o2_scales[:, P * h : P * (h + 1)],
+                        rhs=w2[:, h, cols].bitcast(FP8X4),
+                        rhs_scale=w2_scales[LIVE * h : P, cols],
+                        start=(h == 0),
+                        stop=(h == PASSES2 - 1),
+                    )
+            return banks
 
-        def finish(n, banks):
-            share = BANK // OCTET
-            for k in range(RUN_BANKS):
-                total = addend[:, n, :, share * k : share * (k + 1)]
+        def finish(c, o3_ps):
+            o3_sorted = work.tile([P, PAIRS, 2, P], F32, name="o3_sorted", bufs=2 * RUN)
+            nc.scalar.copy(out=o3_sorted[:], in_=o3_ps[:].rearrange("m (a o r) -> m a r o", a=PAIRS, r=2))
+            o3t_ps = psum_plain.tile([P, PAIRS, 2, P], F32, name="o3t_ps", tag="plain")
+            for a in range(PAIRS):
+                for r in range(2):
+                    nc.tensor.transpose(o3t_ps[:, a, r, :], o3_sorted[:, a, r, :], ident_f32[:])
+            for a in range(PAIRS):
+                G = PAIRS * c + a
                 nc.vector.tensor_tensor(
-                    out=total, in0=banks[k][:].rearrange("m (p r) -> m r p", r=OCTET), in1=total, op=ADD
+                    out=result[:, G, :, :, :],
+                    in0=o3t_ps[:, a, :, :].rearrange("p r (b s) -> p b r s", b=BATCH),
+                    in1=result[:, G, :, :, :],
+                    op=ADD,
                 )
-            result = work.tile([P, BATCH, OCTET, SPOTS], F32, name="result")
-            planes = BANK // P
-            for k in range(RUN_BANKS):
-                o3t_ps = psum_plain.tile([P, planes, P], F32, name="o3t_ps", tag="plain")
-                for r in range(planes):
-                    nc.tensor.transpose(o3t_ps[:, r, :], addend[:, n, planes * k + r, :], ident_f32[:])
-                nc.scalar.copy(
-                    out=result[:, :, planes * k : planes * (k + 1), :],
-                    in_=o3t_ps[:].rearrange("p r (b s) -> p b r s", b=BATCH),
-                )
-            for b in range(BATCH):
-                nc.sync.dma_start(out=out_by_octet[:, n, b, :], in_=result[:, b, :, :].rearrange("p r s -> p (r s)"))
+                nc.sync.dma_start(out=out_by_pair[:, G, :, :], in_=result[:, G, :, :, :].rearrange("p b r s -> p b (r s)"))
 
-        ahead = [multiply(0, k) for k in range(RUN_BANKS)]
-        for n in range(RUNS):
-            current = ahead
-            if n + 1 < RUNS:
-                ahead = [multiply(n + 1, k) for k in range(RUN_BANKS)]
-            finish(n, current)
+        banks = multiply(range(2 * RUN))
+        for first in range(0, CHUNKS, RUN):
+            for c in range(first, first + RUN):
+                finish(c, banks[c])
+            if first + 2 * RUN < CHUNKS:
+                banks.extend(multiply(range(first + 2 * RUN, first + 3 * RUN)))

@@ -25,10 +25,11 @@ PASSES2 = HID // (P * PACK)
 QUAD = 4
 QUADS = PASSES1 // QUAD
 LIVE = 4
-W2_LOADS = 4
-CHUNKS = OC // BANK
-PAIRS = BANK // (2 * P)
-RUN = 2
+NEAR = 4
+RANGES = OC // BANK
+W2_COLS = 2 * BANK
+PAIR = 2
+RUN = 4
 
 FLOPS = 2 * P * (CHANNELS * PACK) * HID + 2 * P * HID * OC
 
@@ -55,30 +56,29 @@ def tile_memoryefficientpatchdownscale_k_kernel(
         w1_scales = keep.tile([P, QUADS, HID], U8, align_bytes=64)
         w2_scales = keep.tile([P, OC], U8, align_bytes=64)
         bias1_row = keep.tile([P, HID], BF16)
-        bias2_rows = keep.tile([P, 2 * P], BF16)
+        bias2_rows = keep.tile([P, BANK], BF16)
         ones = keep.tile([P, P], BF16)
         ident_bf16 = keep.tile([P, P], BF16)
         ident_f32 = keep.tile([P, P], F32)
         bias1_all = keep.tile([P, PASSES2, PACK, P], F32)
-        bias2_cols = keep.tile([P, PASSES1, 2], F32)
+        bias2_cols = keep.tile([P, RANGES, NEAR], F32)
         zero_col = keep.tile([P, 1], F32)
         silu_col = keep.tile([P, 1], F32)
         patch_sums = keep.tile([P, PASSES1 * P], F32)
-        result = keep.tile([P, PASSES1, BATCH, 2, SPOTS], F32)
+        result = keep.tile([P, RANGES, BATCH, NEAR, SPOTS], F32)
         o2_codes = keep.tile([P, PASSES2 * P], I32, align_bytes=64)
         o2_scales = keep.tile([P, PASSES2 * P], U8, align_bytes=64)
 
-        nc.vector.memset(w1_scales[:].rearrange("p q n -> p (q n)").bitcast(I32), 0)
-        nc.vector.memset(w2_scales[:].bitcast(I32), 0)
+        for q in range(QUADS):
+            nc.vector.memset(w1_scales[:, q, :].bitcast(I32), 0)
         nc.vector.memset(zero_col[:], 0.0)
         nc.vector.memset(bias1_row[:], 0.0)
         nc.vector.memset(bias2_rows[:], 0.0)
         nc.vector.memset(ones[:], 1.0)
-        make_identity(nc, ident_bf16[:])
-        make_identity(nc, ident_f32[:])
+        nc.vector.memset(w2_scales[:].bitcast(I32), 0)
 
         nc.scalar.dma_start(out=bias1_row[0:1, :], in_=bias1.rearrange("(o n) -> o n", o=1))
-        nc.scalar.dma_start(out=bias2_rows[0:PASSES1, :], in_=bias2.rearrange("(g c) -> g c", c=2 * P))
+        nc.scalar.dma_start(out=bias2_rows[0:RANGES, :], in_=bias2.rearrange("(m c) -> m c", c=BANK))
         nc.scalar.activation(out=silu_col[:], in_=zero_col[:], func=ACT.Silu)
 
         x_by_channel = x.rearrange("b (g p) h w -> p g b (h w)", p=P)
@@ -88,12 +88,13 @@ def tile_memoryefficientpatchdownscale_k_kernel(
         for g in range(PASSES1):
             nc.sync.dma_start(out=w1[:, g, :], in_=weight1_words[g].rearrange("p n t -> p (n t)").bitcast(I32))
         w2_bytes = weight2_words.rearrange("g p n t -> p g (n t)")
-        w2_cols = OC // W2_LOADS
-        for n in range(W2_LOADS):
-            nc.sync.dma_start(
-                out=w2[:, :, w2_cols * n : w2_cols * (n + 1)],
-                in_=w2_bytes[:, :, PACK * w2_cols * n : PACK * w2_cols * (n + 1)].bitcast(I32),
-            )
+        for n in range(OC // W2_COLS):
+            both = n < OC // W2_COLS - 1
+            for passes in [slice(0, 2)] if both else [slice(0, 1), slice(1, 2)]:
+                nc.sync.dma_start(
+                    out=w2[:, passes, W2_COLS * n : W2_COLS * (n + 1)],
+                    in_=w2_bytes[:, passes, PACK * W2_COLS * n : PACK * W2_COLS * (n + 1)].bitcast(I32),
+                )
 
         for q in range(QUADS):
             for Q in range(4):
@@ -101,6 +102,9 @@ def tile_memoryefficientpatchdownscale_k_kernel(
                     out=w1_scales[32 * Q : 32 * Q + QUAD * LIVE, q, :].bitcast(F32),
                     in_=weight1_scales[QUAD * q : QUAD * (q + 1), LIVE * Q : LIVE * (Q + 1), :].bitcast(F32),
                 )
+            if q == 1:
+                make_identity(nc, ident_f32[:])
+                make_identity(nc, ident_bf16[:])
         for Q in range(4):
             nc.gpsimd.dma_start(
                 out=w2_scales[32 * Q : 32 * Q + PASSES2 * LIVE, :].bitcast(F32),
@@ -122,13 +126,19 @@ def tile_memoryefficientpatchdownscale_k_kernel(
                 out=bias1_ps[:], lhsT=ones[:], rhs=bias1_row[:, BANK * h : BANK * (h + 1)], start=True, stop=True
             )
             nc.scalar.copy(out=bias1_all[:, h, :, :], in_=bias1_ps[:].rearrange("m (p t) -> m t p", t=PACK))
-        bias2_ps = psum_plain.tile([P, 2, P], BF16, tag="plain")
-        for r in range(2):
-            nc.tensor.transpose(bias2_ps[:, r, :], bias2_rows[:, r : 2 * P : 2], ident_bf16[:])
-        nc.vector.tensor_copy(out=bias2_cols[:], in_=bias2_ps[:, :, 0:PASSES1].rearrange("p r g -> p g r"))
+
+        for q in range(QUADS):
+            nc.vector.tensor_reduce(
+                out=patch_sums[:, QUAD * P * q : QUAD * P * (q + 1)],
+                in_=patches[q][:].rearrange("p (c t) -> p c t", t=PACK),
+                axis=mybir.AxisListType.X,
+                op=ADD,
+            )
 
         o1_ps = [psum_mx.tile([P, BANK], F32, name="o1_ps%d" % h, tag="mx") for h in range(PASSES2)]
-        for g in range(PASSES1):
+        sums_sorted = {}
+
+        def multiply1(g):
             first_row = LIVE * (g % QUAD)
             for h in range(PASSES2):
                 cols = slice(BANK * h, BANK * (h + 1))
@@ -142,22 +152,45 @@ def tile_memoryefficientpatchdownscale_k_kernel(
                     stop=(g == PASSES1 - 1),
                 )
 
-        for q in range(QUADS):
-            nc.vector.tensor_reduce(
-                out=patch_sums[:, QUAD * P * q : QUAD * P * (q + 1)],
-                in_=patches[q][:].rearrange("p (c t) -> p c t", t=PACK),
-                axis=mybir.AxisListType.X,
-                op=ADD,
-            )
-            for G in range(QUAD * q, QUAD * (q + 1)):
-                for r in range(2):
+        def spread_bias2():
+            bias2_ps = psum_plain.tile([P, NEAR, P], BF16, name="bias2_ps", tag="plain")
+            for r in range(NEAR):
+                nc.tensor.transpose(bias2_ps[:, r, :], bias2_rows[:, r:BANK:NEAR], ident_bf16[:])
+            nc.scalar.copy(out=bias2_cols[:], in_=bias2_ps[:, :, 0:RANGES].rearrange("p r m -> p m r"))
+
+        def sums_to_patches(q):
+            sums_ps = psum_plain.tile([P, QUAD * P], F32, name="sums_ps", tag="plain")
+            for g in range(QUAD):
+                cols = slice(P * (QUAD * q + g), P * (QUAD * q + g + 1))
+                nc.tensor.transpose(sums_ps[:, P * g : P * (g + 1)], patch_sums[:, cols], ident_f32[:])
+            sums_sorted[q] = work.tile([P, 2, 2, P], F32, name="sums_sorted")
+            nc.scalar.copy(out=sums_sorted[q][:], in_=sums_ps[:].rearrange("s (a p j) -> s a j p", a=2, j=2))
+
+        def sums_to_channels(q):
+            pooled_ps = psum_plain.tile([P, 2, 2, P], F32, name="pooled_ps", tag="plain")
+            for a in range(2):
+                for j in range(2):
+                    nc.tensor.transpose(pooled_ps[:, a, j, :], sums_sorted[q][:, a, j, :], ident_f32[:])
+            for a in range(2):
+                for r in range(NEAR):
                     nc.scalar.activation(
-                        out=result[:, G, :, r, :],
-                        in_=patch_sums[:, P * G : P * (G + 1)].rearrange("p (b s) -> p b s", b=BATCH),
+                        out=result[:, 2 * q + a, :, r, :],
+                        in_=pooled_ps[:, a, r // 2, :].rearrange("p (b s) -> p b s", b=BATCH),
                         func=ACT.Identity,
-                        bias=bias2_cols[:, G, r : r + 1],
+                        bias=bias2_cols[:, 2 * q + a, r : r + 1],
                         scale=1.0 / PACK,
                     )
+
+        for g in range(PASSES1):
+            multiply1(g)
+            if g % 2 == 1:
+                q = g // 2 - 1
+                if q == 0:
+                    spread_bias2()
+                if 0 <= q < QUADS:
+                    sums_to_patches(q)
+                if 1 <= q <= QUADS:
+                    sums_to_channels(q - 1)
 
         halves = range(PASSES2)
         o1_sorted = [work.tile([P, PACK, P], F32, name="o1_sorted") for h in halves]
@@ -184,44 +217,57 @@ def tile_memoryefficientpatchdownscale_k_kernel(
                 in_=o2_words[h][:].rearrange("p m t -> p (m t)"),
             )
 
-        out_by_pair = out.rearrange("b (g o r) i j -> o g b (r i j)", o=P, r=2)
+        out_by_run = out.rearrange("b (m p r) i j -> p m b (r i j)", p=P, r=NEAR)
+        o3_ps = {}
+        o3_sorted = {}
 
-        def multiply(chunks):
-            banks = [psum_mx.tile([P, BANK], F32, name="o3_ps", tag="mx") for c in chunks]
+        def multiply2(m, h):
+            if h == 0:
+                o3_ps[m] = psum_mx.tile([P, BANK], F32, name="o3_ps", tag="mx")
+            cols = slice(BANK * m, BANK * (m + 1))
+            nc.tensor.matmul_mx(
+                out=o3_ps[m][:],
+                lhsT=o2_codes[:, P * h : P * (h + 1)].bitcast(FP8X4),
+                lhsT_scale=o2_scales[:, P * h : P * (h + 1)],
+                rhs=w2[:, h, cols].bitcast(FP8X4),
+                rhs_scale=w2_scales[LIVE * h : P, cols],
+                start=(h == 0),
+                stop=(h == PASSES2 - 1),
+            )
+
+        def take_out(m):
+            o3_sorted[m] = work.tile([P, NEAR, P], F32, name="o3_sorted", bufs=RUN)
+            nc.scalar.copy(out=o3_sorted[m][:], in_=o3_ps[m][:].rearrange("s (p r) -> s r p", r=NEAR))
+
+        def finish(m):
+            o3t_ps = psum_plain.tile([P, NEAR, P], F32, name="o3t_ps", tag="plain")
+            for r in range(NEAR):
+                nc.tensor.transpose(o3t_ps[:, r, :], o3_sorted[m][:, r, :], ident_f32[:])
+            nc.vector.tensor_tensor(
+                out=result[:, m, :, :, :],
+                in0=o3t_ps[:].rearrange("p r (b s) -> p b r s", b=BATCH),
+                in1=result[:, m, :, :, :],
+                op=ADD,
+            )
+            nc.sync.dma_start(out=out_by_run[:, m, :, :], in_=result[:, m, :, :, :].rearrange("p b r s -> p b (r s)"))
+
+        last = RANGES - PAIR
+        for first in range(0, last, PAIR):
             for h in range(PASSES2):
-                for c, o3_ps in zip(chunks, banks):
-                    cols = slice(BANK * c, BANK * (c + 1))
-                    nc.tensor.matmul_mx(
-                        out=o3_ps[:],
-                        lhsT=o2_codes[:, P * h : P * (h + 1)].bitcast(FP8X4),
-                        lhsT_scale=o2_scales[:, P * h : P * (h + 1)],
-                        rhs=w2[:, h, cols].bitcast(FP8X4),
-                        rhs_scale=w2_scales[LIVE * h : P, cols],
-                        start=(h == 0),
-                        stop=(h == PASSES2 - 1),
-                    )
-            return banks
-
-        def finish(c, o3_ps):
-            o3_sorted = work.tile([P, PAIRS, 2, P], F32, name="o3_sorted", bufs=2 * RUN)
-            nc.scalar.copy(out=o3_sorted[:], in_=o3_ps[:].rearrange("m (a o r) -> m a r o", a=PAIRS, r=2))
-            o3t_ps = psum_plain.tile([P, PAIRS, 2, P], F32, name="o3t_ps", tag="plain")
-            for a in range(PAIRS):
-                for r in range(2):
-                    nc.tensor.transpose(o3t_ps[:, a, r, :], o3_sorted[:, a, r, :], ident_f32[:])
-            for a in range(PAIRS):
-                G = PAIRS * c + a
-                nc.vector.tensor_tensor(
-                    out=result[:, G, :, :, :],
-                    in0=o3t_ps[:, a, :, :].rearrange("p r (b s) -> p b r s", b=BATCH),
-                    in1=result[:, G, :, :, :],
-                    op=ADD,
-                )
-                nc.sync.dma_start(out=out_by_pair[:, G, :, :], in_=result[:, G, :, :, :].rearrange("p b r s -> p b (r s)"))
-
-        banks = multiply(range(2 * RUN))
-        for first in range(0, CHUNKS, RUN):
-            for c in range(first, first + RUN):
-                finish(c, banks[c])
-            if first + 2 * RUN < CHUNKS:
-                banks.extend(multiply(range(first + 2 * RUN, first + 3 * RUN)))
+                for m in range(first, first + PAIR):
+                    multiply2(m, h)
+            for m in range(first, first + PAIR):
+                take_out(m)
+            if first == RUN - PAIR:
+                for m in range(RUN):
+                    finish(m)
+        for m in range(last, RANGES):
+            multiply2(m, 0)
+        multiply2(last, 1)
+        take_out(last)
+        for m in range(last - PAIR, last):
+            finish(m)
+        multiply2(last + 1, 1)
+        take_out(last + 1)
+        for m in range(last, RANGES):
+            finish(m)

from contextlib import ExitStack

import concourse.mybir as mybir
from concourse.masks import make_identity

F32 = mybir.dt.float32
BF16 = mybir.dt.bfloat16
I32 = mybir.dt.int32
U8 = mybir.dt.uint8
FP8X4 = mybir.dt.float8_e4m3fn_x4
ADD = mybir.AluOpType.add
ACT = mybir.ActivationFunctionType

P = 128
PACK = 4
BANK = 512
BATCH = 2
CHANNELS = 2048
PIXELS = 256
SPOTS = 64
HID = 1024
OC = 4096
PASSES1 = CHANNELS // P
PASSES2 = HID // (P * PACK)
QUAD = 4
QUADS = PASSES1 // QUAD
LIVE = 4
NEAR = 4
RANGES = OC // BANK
W2_COLS = 2 * BANK
PAIR = 2
RUN = 4

FLOPS = 2 * P * (CHANNELS * PACK) * HID + 2 * P * HID * OC


def tile_memoryefficientpatchdownscale_k_kernel(
    tc, x, weight1_words, weight1_scales, bias1, weight2_words, weight2_scales, bias2, out
):
    nc = tc.nc
    with ExitStack() as ctx:
        keep = ctx.enter_context(tc.tile_pool(name="keep", bufs=1))
        work = ctx.enter_context(tc.tile_pool(name="work", bufs=2))
        psum_mx = ctx.enter_context(tc.psum_pool(name="psum_mx", bufs=4))
        psum_plain = ctx.enter_context(tc.psum_pool(name="psum_plain", bufs=4))
        ctx.enter_context(tc.manual_schedule())

        x_quads = [keep.tile([P, QUAD, BATCH, PIXELS], BF16, name="x_quad%d" % q) for q in range(QUADS)]
        patches = [
            keep.tile([P, QUAD * P * PACK], BF16, name="patches%d" % q, align_bytes=64) for q in range(QUADS)
        ]
        x_codes = keep.tile([P, PASSES1 * P], I32, align_bytes=64)
        x_scales = keep.tile([P, PASSES1 * P], U8, align_bytes=64)
        w1 = keep.tile([P, PASSES1, HID], I32, align_bytes=64)
        w2 = keep.tile([P, PASSES2, OC], I32, align_bytes=64)
        w1_scales = keep.tile([P, QUADS, HID], U8, align_bytes=64)
        w2_scales = keep.tile([P, OC], U8, align_bytes=64)
        bias1_row = keep.tile([P, HID], BF16)
        bias2_rows = keep.tile([P, BANK], BF16)
        ones = keep.tile([P, P], BF16)
        ident_bf16 = keep.tile([P, P], BF16)
        ident_f32 = keep.tile([P, P], F32)
        bias1_all = keep.tile([P, PASSES2, PACK, P], F32)
        bias2_cols = keep.tile([P, RANGES, NEAR], F32)
        zero_col = keep.tile([P, 1], F32)
        silu_col = keep.tile([P, 1], F32)
        patch_sums = keep.tile([P, PASSES1 * P], F32)
        result = keep.tile([P, RANGES, BATCH, NEAR, SPOTS], F32)
        o2_codes = keep.tile([P, PASSES2 * P], I32, align_bytes=64)
        o2_scales = keep.tile([P, PASSES2 * P], U8, align_bytes=64)

        for q in range(QUADS):
            nc.vector.memset(w1_scales[:, q, :].bitcast(I32), 0)
        nc.vector.memset(zero_col[:], 0.0)
        nc.vector.memset(bias1_row[:], 0.0)
        nc.vector.memset(bias2_rows[:], 0.0)
        nc.vector.memset(ones[:], 1.0)
        nc.vector.memset(w2_scales[:].bitcast(I32), 0)

        nc.scalar.dma_start(out=bias1_row[0:1, :], in_=bias1.rearrange("(o n) -> o n", o=1))
        nc.scalar.dma_start(out=bias2_rows[0:RANGES, :], in_=bias2.rearrange("(m c) -> m c", c=BANK))
        nc.scalar.activation(out=silu_col[:], in_=zero_col[:], func=ACT.Silu)

        x_by_channel = x.rearrange("b (g p) h w -> p g b (h w)", p=P)
        for q in range(QUADS):
            for b in range(BATCH):
                nc.sync.dma_start(out=x_quads[q][:, :, b, :], in_=x_by_channel[:, QUAD * q : QUAD * (q + 1), b, :])
        for g in range(PASSES1):
            nc.sync.dma_start(out=w1[:, g, :], in_=weight1_words[g].rearrange("p n t -> p (n t)").bitcast(I32))
        w2_bytes = weight2_words.rearrange("g p n t -> p g (n t)")
        for n in range(OC // W2_COLS):
            both = n < OC // W2_COLS - 1
            for passes in [slice(0, 2)] if both else [slice(0, 1), slice(1, 2)]:
                nc.sync.dma_start(
                    out=w2[:, passes, W2_COLS * n : W2_COLS * (n + 1)],
                    in_=w2_bytes[:, passes, PACK * W2_COLS * n : PACK * W2_COLS * (n + 1)].bitcast(I32),
                )

        for q in range(QUADS):
            for Q in range(4):
                nc.gpsimd.dma_start(
                    out=w1_scales[32 * Q : 32 * Q + QUAD * LIVE, q, :].bitcast(F32),
                    in_=weight1_scales[QUAD * q : QUAD * (q + 1), LIVE * Q : LIVE * (Q + 1), :].bitcast(F32),
                )
            if q == 1:
                make_identity(nc, ident_f32[:])
                make_identity(nc, ident_bf16[:])
        for Q in range(4):
            nc.gpsimd.dma_start(
                out=w2_scales[32 * Q : 32 * Q + PASSES2 * LIVE, :].bitcast(F32),
                in_=weight2_scales[:, LIVE * Q : LIVE * (Q + 1), :].bitcast(F32),
            )

        for q in range(QUADS):
            pixel_pairs = x_quads[q][:].rearrange("p g b f -> p (g b f)").bitcast(F32)
            nc.vector.tensor_copy(
                out=patches[q][:].bitcast(F32).rearrange("p (a j u) -> p a j u", j=8, u=2),
                in_=pixel_pairs.rearrange("p (a u j) -> p a j u", u=2, j=8),
            )
            cols = slice(QUAD * P * q, QUAD * P * (q + 1))
            nc.vector.quantize_mx(out=x_codes[:, cols].bitcast(FP8X4), scales=x_scales[:, cols], in_=patches[q][:])

        for h in range(PASSES2):
            bias1_ps = psum_plain.tile([P, BANK], F32, tag="plain")
            nc.tensor.matmul(
                out=bias1_ps[:], lhsT=ones[:], rhs=bias1_row[:, BANK * h : BANK * (h + 1)], start=True, stop=True
            )
            nc.scalar.copy(out=bias1_all[:, h, :, :], in_=bias1_ps[:].rearrange("m (p t) -> m t p", t=PACK))

        for q in range(QUADS):
            nc.vector.tensor_reduce(
                out=patch_sums[:, QUAD * P * q : QUAD * P * (q + 1)],
                in_=patches[q][:].rearrange("p (c t) -> p c t", t=PACK),
                axis=mybir.AxisListType.X,
                op=ADD,
            )

        o1_ps = [psum_mx.tile([P, BANK], F32, name="o1_ps%d" % h, tag="mx") for h in range(PASSES2)]
        sums_sorted = {}

        def multiply1(g):
            first_row = LIVE * (g % QUAD)
            for h in range(PASSES2):
                cols = slice(BANK * h, BANK * (h + 1))
                nc.tensor.matmul_mx(
                    out=o1_ps[h][:],
                    lhsT=x_codes[:, P * g : P * (g + 1)].bitcast(FP8X4),
                    lhsT_scale=x_scales[:, P * g : P * (g + 1)],
                    rhs=w1[:, g, cols].bitcast(FP8X4),
                    rhs_scale=w1_scales[first_row:P, g // QUAD, cols],
                    start=(g == 0),
                    stop=(g == PASSES1 - 1),
                )

        def spread_bias2():
            bias2_ps = psum_plain.tile([P, NEAR, P], BF16, name="bias2_ps", tag="plain")
            for r in range(NEAR):
                nc.tensor.transpose(bias2_ps[:, r, :], bias2_rows[:, r:BANK:NEAR], ident_bf16[:])
            nc.scalar.copy(out=bias2_cols[:], in_=bias2_ps[:, :, 0:RANGES].rearrange("p r m -> p m r"))

        def sums_to_patches(q):
            sums_ps = psum_plain.tile([P, QUAD * P], F32, name="sums_ps", tag="plain")
            for g in range(QUAD):
                cols = slice(P * (QUAD * q + g), P * (QUAD * q + g + 1))
                nc.tensor.transpose(sums_ps[:, P * g : P * (g + 1)], patch_sums[:, cols], ident_f32[:])
            sums_sorted[q] = work.tile([P, 2, 2, P], F32, name="sums_sorted")
            nc.scalar.copy(out=sums_sorted[q][:], in_=sums_ps[:].rearrange("s (a p j) -> s a j p", a=2, j=2))

        def sums_to_channels(q):
            pooled_ps = psum_plain.tile([P, 2, 2, P], F32, name="pooled_ps", tag="plain")
            for a in range(2):
                for j in range(2):
                    nc.tensor.transpose(pooled_ps[:, a, j, :], sums_sorted[q][:, a, j, :], ident_f32[:])
            for a in range(2):
                for r in range(NEAR):
                    nc.scalar.activation(
                        out=result[:, 2 * q + a, :, r, :],
                        in_=pooled_ps[:, a, r // 2, :].rearrange("p (b s) -> p b s", b=BATCH),
                        func=ACT.Identity,
                        bias=bias2_cols[:, 2 * q + a, r : r + 1],
                        scale=1.0 / PACK,
                    )

        for g in range(PASSES1):
            multiply1(g)
            if g % 2 == 1:
                q = g // 2 - 1
                if q == 0:
                    spread_bias2()
                if 0 <= q < QUADS:
                    sums_to_patches(q)
                if 1 <= q <= QUADS:
                    sums_to_channels(q - 1)

        halves = range(PASSES2)
        o1_sorted = [work.tile([P, PACK, P], F32, name="o1_sorted") for h in halves]
        o2_sorted = [work.tile([P, PACK, P], BF16, name="o2_sorted") for h in halves]
        o2t_ps = [psum_plain.tile([P, PACK, P], BF16, name="o2t_ps", tag="plain") for h in halves]
        o2_words = [work.tile([P, P, PACK], BF16, name="o2_words", align_bytes=64) for h in halves]
        for h in halves:
            nc.vector.tensor_tensor(
                out=o1_sorted[h][:],
                in0=o1_ps[h][:].rearrange("m (p t) -> m t p", t=PACK),
                in1=bias1_all[:, h, :, :],
                op=ADD,
            )
        for h in halves:
            nc.scalar.activation(out=o2_sorted[h][:], in_=o1_sorted[h][:], func=ACT.Silu)
        for h in halves:
            for t in range(PACK):
                nc.tensor.transpose(o2t_ps[h][:, t, :], o2_sorted[h][:, t, :], ident_bf16[:])
        for h in halves:
            nc.vector.tensor_copy(out=o2_words[h][:], in_=o2t_ps[h][:].rearrange("p t m -> p m t"))
            nc.vector.quantize_mx(
                out=o2_codes[:, P * h : P * (h + 1)].bitcast(FP8X4),
                scales=o2_scales[:, P * h : P * (h + 1)],
                in_=o2_words[h][:].rearrange("p m t -> p (m t)"),
            )

        out_by_run = out.rearrange("b (m p r) i j -> p m b (r i j)", p=P, r=NEAR)
        o3_ps = {}
        o3_sorted = {}

        def multiply2(m, h):
            if h == 0:
                o3_ps[m] = psum_mx.tile([P, BANK], F32, name="o3_ps", tag="mx")
            cols = slice(BANK * m, BANK * (m + 1))
            nc.tensor.matmul_mx(
                out=o3_ps[m][:],
                lhsT=o2_codes[:, P * h : P * (h + 1)].bitcast(FP8X4),
                lhsT_scale=o2_scales[:, P * h : P * (h + 1)],
                rhs=w2[:, h, cols].bitcast(FP8X4),
                rhs_scale=w2_scales[LIVE * h : P, cols],
                start=(h == 0),
                stop=(h == PASSES2 - 1),
            )

        def take_out(m):
            o3_sorted[m] = work.tile([P, NEAR, P], F32, name="o3_sorted", bufs=RUN)
            nc.scalar.copy(out=o3_sorted[m][:], in_=o3_ps[m][:].rearrange("s (p r) -> s r p", r=NEAR))

        def finish(m):
            o3t_ps = psum_plain.tile([P, NEAR, P], F32, name="o3t_ps", tag="plain")
            for r in range(NEAR):
                nc.tensor.transpose(o3t_ps[:, r, :], o3_sorted[m][:, r, :], ident_f32[:])
            nc.vector.tensor_tensor(
                out=result[:, m, :, :, :],
                in0=o3t_ps[:].rearrange("p r (b s) -> p b r s", b=BATCH),
                in1=result[:, m, :, :, :],
                op=ADD,
            )
            nc.sync.dma_start(out=out_by_run[:, m, :, :], in_=result[:, m, :, :, :].rearrange("p b r s -> p b (r s)"))

        last = RANGES - PAIR
        for first in range(0, last, PAIR):
            for h in range(PASSES2):
                for m in range(first, first + PAIR):
                    multiply2(m, h)
            for m in range(first, first + PAIR):
                take_out(m)
            if first == RUN - PAIR:
                for m in range(RUN):
                    finish(m)
        for m in range(last, RANGES):
            multiply2(m, 0)
        multiply2(last, 1)
        take_out(last)
        for m in range(last - PAIR, last):
            finish(m)
        multiply2(last + 1, 1)
        take_out(last + 1)
        for m in range(last, RANGES):
            finish(m)
